import numpy as np
import ml_dtypes

BF16 = ml_dtypes.bfloat16


def bf(x):
    return np.asarray(x, np.float32).astype(BF16)


def f32(x):
    return np.asarray(x, np.float32)


def f64(x):
    return np.asarray(x).astype(np.float64)


def striped(idx):
    return np.tile(idx.reshape(-1, 16).T, (8, 1))


D, H, HD, HALF, C, S, N = 512, 4, 128, 64, 1024, 4096, 2048
THETA = 10000.0


def turn(t):
    r = t.reshape(H, -1, HALF, t.shape[-1])
    return np.concatenate((-r[:, 1:], r[:, :1]), axis=1).reshape(t.shape)


def angles():
    inv = 1.0 / THETA ** (np.arange(HALF) / HALF)
    fr = np.outer(inv, np.arange(N)).astype(np.float32)
    return np.concatenate((fr, fr), axis=0)


def setup_inputs():
    a = angles()
    return {"x": bf(np.random.standard_normal((D, N))), "wq": bf(np.random.standard_normal((D, D)) / np.sqrt(D)), "wk": bf(np.random.standard_normal((D, D)) / np.sqrt(D)), "cos_pos": f32(np.cos(a)), "sin_pos": f32(np.sin(a)), "base": f32(np.random.standard_normal((C, S))), "offs": striped(np.random.permutation(S)[:N])}


def reference(x, wq, wk, cos_pos, sin_pos, base, offs):
    idx = offs[:16].T.reshape(-1)
    xx = f64(x)
    cc = np.tile(f64(cos_pos), (H, 1))
    ss = np.tile(f64(sin_pos), (H, 1))
    res = f64(base).copy()
    res[:D, idx] = (f64(wq).T @ xx) * cc + (turn(f64(wq).T) @ xx) * ss
    res[D:, idx] = (f64(wk).T @ xx) * cc + (turn(f64(wk).T) @ xx) * ss
    return res

@@ -1,0 +1,80 @@
+import concourse.mybir as mybir
+
+BF16, F32, U16 = mybir.dt.bfloat16, mybir.dt.float32, mybir.dt.uint16
+MULT, ADD = mybir.AluOpType.mult, mybir.AluOpType.add
+COPY = mybir.ActivationFunctionType.Copy
+
+P = 128
+D = 512
+HALF = 64
+N = 2048
+S = 4096
+K_BLOCKS = D // P
+HEADS = D // P
+CHUNK = 512
+CHUNKS = N // CHUNK
+
+FLOPS = 2 * D * (2 * D) * N + 3 * (2 * D) * N
+
+
+def tile_flaxllamaattention_b_kernel(tc, x, wq, wk, cos_pos, sin_pos, base, offs, out):
+    nc = tc.nc
+    with (
+        tc.tile_pool(name="held", bufs=1) as held,
+        tc.tile_pool(name="windows", bufs=4) as windows,
+        tc.tile_pool(name="products", bufs=2) as products,
+        tc.psum_pool(name="banks", bufs=8) as banks,
+    ):
+        offsets = held.tile([P, N // 16], U16, name="offsets")
+        nc.sync.dma_start(offsets[:], offs)
+
+        x_sb = held.tile([P, K_BLOCKS, N], BF16, name="x_sb")
+        cos_sb = held.tile([P, N], F32, name="cos_sb")
+        sin_sb = held.tile([P, N], F32, name="sin_sb")
+        wq_sb = held.tile([P, K_BLOCKS, D], BF16, name="wq_sb")
+        wk_sb = held.tile([P, K_BLOCKS, D], BF16, name="wk_sb")
+        wq_turned = held.tile([P, K_BLOCKS, D], BF16, name="wq_turned")
+        wk_turned = held.tile([P, K_BLOCKS, D], BF16, name="wk_turned")
+
+        x_blocks = x.rearrange("(k p) n -> p k n", p=P)
+        nc.scalar.dma_start(wq_sb[:], wq.rearrange("(k p) c -> p k c", p=P))
+        for chunk in range(CHUNKS):
+            tokens = slice(chunk * CHUNK, (chunk + 1) * CHUNK)
+            nc.sync.dma_start(x_sb[:, :, tokens], x_blocks[:, :, tokens])
+            nc.scalar.dma_start(cos_sb[:, tokens], cos_pos[:, tokens])
+            nc.scalar.dma_start(sin_sb[:, tokens], sin_pos[:, tokens])
+        nc.scalar.dma_start(wk_sb[:], wk.rearrange("(k p) c -> p k c", p=P))
+
+        for plain, turned in ((wq_sb, wq_turned), (wk_sb, wk_turned)):
+            source = plain[:].rearrange("p k (h t e) -> p (k h) t e", t=2, e=HALF)
+            landing = turned[:].rearrange("p k (h t e) -> p (k h) t e", t=2, e=HALF)
+            nc.scalar.activation(landing[:, :, 0, :], source[:, :, 1, :], COPY, scale=-1.0)
+            nc.scalar.activation(landing[:, :, 1, :], source[:, :, 0, :], COPY)
+
+        blocks = [(wq_sb, wq_turned, head) for head in range(HEADS)]
+        blocks += [(wk_sb, wk_turned, head) for head in range(HEADS)]
+        for block, (plain, turned, head) in enumerate(blocks):
+            rows = slice(block * P, (block + 1) * P)
+            channels = slice(head * P, (head + 1) * P)
+
+            window = windows.tile([P, S], F32, name="window")
+            nc.sync.dma_start(window[:], base[rows, :])
+
+            with_cos = products.tile([P, N], F32, name="with_cos")
+            with_sin = products.tile([P, N], F32, name="with_sin")
+            for chunk in range(CHUNKS):
+                tokens = slice(chunk * CHUNK, (chunk + 1) * CHUNK)
+                for weights, table, product in ((plain, cos_sb, with_cos), (turned, sin_sb, with_sin)):
+                    projected = banks.tile([P, CHUNK], F32, name="projected")
+                    for k in range(K_BLOCKS):
+                        nc.tensor.matmul(
+                            projected[:],
+                            weights[:, k, channels],
+                            x_sb[:, k, tokens],
+                            start=(k == 0),
+                            stop=(k == K_BLOCKS - 1),
+                        )
+                    nc.vector.tensor_tensor(product[:, tokens], projected[:], table[:, tokens], MULT)
+
+            nc.vector.tensor_tensor(window[:].indirect(offsets[:]), with_cos[:], with_sin[:], ADD)
+            nc.scalar.dma_start(out[rows, :], window[:])

@@ -11,18 +11,26 @@ N = 2048
 S = 4096
 K_BLOCKS = D // P
 HEADS = D // P
+BLOCKS = 2 * HEADS
 CHUNK = 512
 CHUNKS = N // CHUNK
+AHEAD = 3
 
 FLOPS = 2 * D * (2 * D) * N + 3 * (2 * D) * N
+
+
+def load_window(nc, windows, base, block):
+    window = windows.tile([P, S], F32, name="window")
+    nc.sync.dma_start(window[:], base[block * P : (block + 1) * P, :])
+    return window
 
 
 def tile_flaxllamaattention_b_kernel(tc, x, wq, wk, cos_pos, sin_pos, base, offs, out):
     nc = tc.nc
     with (
         tc.tile_pool(name="held", bufs=1) as held,
-        tc.tile_pool(name="windows", bufs=4) as windows,
-        tc.tile_pool(name="products", bufs=2) as products,
+        tc.tile_pool(name="windows", bufs=AHEAD + 1) as windows,
+        tc.tile_pool(name="staged", bufs=4) as staged,
         tc.psum_pool(name="banks", bufs=8) as banks,
     ):
         offsets = held.tile([P, N // 16], U16, name="offsets")
@@ -37,44 +45,49 @@ def tile_flaxllamaattention_b_kernel(tc, x, wq, wk, cos_pos, sin_pos, base, offs
         wk_turned = held.tile([P, K_BLOCKS, D], BF16, name="wk_turned")
 
         x_blocks = x.rearrange("(k p) n -> p k n", p=P)
-        nc.scalar.dma_start(wq_sb[:], wq.rearrange("(k p) c -> p k c", p=P))
+        nc.sync.dma_start(wq_sb[:], wq.rearrange("(k p) c -> p k c", p=P))
         for chunk in range(CHUNKS):
             tokens = slice(chunk * CHUNK, (chunk + 1) * CHUNK)
             nc.sync.dma_start(x_sb[:, :, tokens], x_blocks[:, :, tokens])
-            nc.scalar.dma_start(cos_sb[:, tokens], cos_pos[:, tokens])
-            nc.scalar.dma_start(sin_sb[:, tokens], sin_pos[:, tokens])
-        nc.scalar.dma_start(wk_sb[:], wk.rearrange("(k p) c -> p k c", p=P))
+        nc.sync.dma_start(cos_sb[:], cos_pos)
+        nc.sync.dma_start(sin_sb[:], sin_pos)
+        window_of = {0: load_window(nc, windows, base, 0)}
+        nc.sync.dma_start(wk_sb[:], wk.rearrange("(k p) c -> p k c", p=P))
+        for block in range(1, AHEAD):
+            window_of[block] = load_window(nc, windows, base, block)
 
         for plain, turned in ((wq_sb, wq_turned), (wk_sb, wk_turned)):
             source = plain[:].rearrange("p k (h t e) -> p (k h) t e", t=2, e=HALF)
             landing = turned[:].rearrange("p k (h t e) -> p (k h) t e", t=2, e=HALF)
-            nc.scalar.activation(landing[:, :, 0, :], source[:, :, 1, :], COPY, scale=-1.0)
-            nc.scalar.activation(landing[:, :, 1, :], source[:, :, 0, :], COPY)
+            nc.vector.tensor_scalar_mul(landing[:, :, 0, :], source[:, :, 1, :], -1.0)
+            nc.vector.tensor_copy(landing[:, :, 1, :], source[:, :, 0, :])
 
-        blocks = [(wq_sb, wq_turned, head) for head in range(HEADS)]
-        blocks += [(wk_sb, wk_turned, head) for head in range(HEADS)]
-        for block, (plain, turned, head) in enumerate(blocks):
-            rows = slice(block * P, (block + 1) * P)
+        for block in range(BLOCKS):
+            plain, turned = ((wq_sb, wq_turned), (wk_sb, wk_turned))[block // HEADS]
+            head = block % HEADS
             channels = slice(head * P, (head + 1) * P)
+            if block + AHEAD < BLOCKS:
+                window_of[block + AHEAD] = load_window(nc, windows, base, block + AHEAD)
 
-            window = windows.tile([P, S], F32, name="window")
-            nc.sync.dma_start(window[:], base[rows, :])
-
-            with_cos = products.tile([P, N], F32, name="with_cos")
-            with_sin = products.tile([P, N], F32, name="with_sin")
-            for chunk in range(CHUNKS):
-                tokens = slice(chunk * CHUNK, (chunk + 1) * CHUNK)
-                for weights, table, product in ((plain, cos_sb, with_cos), (turned, sin_sb, with_sin)):
-                    projected = banks.tile([P, CHUNK], F32, name="projected")
+            pair = []
+            for weights, table in ((plain, cos_sb), (turned, sin_sb)):
+                projected = staged.tile([P, N], F32, name="projected")
+                for chunk in range(CHUNKS):
+                    tokens = slice(chunk * CHUNK, (chunk + 1) * CHUNK)
+                    bank = banks.tile([P, CHUNK], F32, name="bank")
                     for k in range(K_BLOCKS):
                         nc.tensor.matmul(
-                            projected[:],
+                            bank[:],
                             weights[:, k, channels],
                             x_sb[:, k, tokens],
                             start=(k == 0),
                             stop=(k == K_BLOCKS - 1),
                         )
-                    nc.vector.tensor_tensor(product[:, tokens], projected[:], table[:, tokens], MULT)
+                    nc.scalar.activation(projected[:, tokens], bank[:], COPY)
+                product = staged.tile([P, N], F32, name="product")
+                nc.gpsimd.tensor_tensor(product[:], projected[:], table[:], MULT)
+                pair.append(product)
 
-            nc.vector.tensor_tensor(window[:].indirect(offsets[:]), with_cos[:], with_sin[:], ADD)
-            nc.scalar.dma_start(out[rows, :], window[:])
+            window = window_of[block]
+            nc.vector.tensor_tensor(window[:].indirect(offsets[:]), pair[0][:], pair[1][:], ADD)
+            nc.sync.dma_start(out[block * P : (block + 1) * P, :], window[:])

@@ -30,7 +30,7 @@ def tile_flaxllamaattention_b_kernel(tc, x, wq, wk, cos_pos, sin_pos, base, offs
     with (
         tc.tile_pool(name="held", bufs=1) as held,
         tc.tile_pool(name="windows", bufs=AHEAD + 1) as windows,
-        tc.tile_pool(name="staged", bufs=4) as staged,
+        tc.tile_pool(name="products", bufs=2) as products,
         tc.psum_pool(name="banks", bufs=8) as banks,
     ):
         offsets = held.tile([P, N // 16], U16, name="offsets")
@@ -49,45 +49,41 @@ def tile_flaxllamaattention_b_kernel(tc, x, wq, wk, cos_pos, sin_pos, base, offs
         for chunk in range(CHUNKS):
             tokens = slice(chunk * CHUNK, (chunk + 1) * CHUNK)
             nc.sync.dma_start(x_sb[:, :, tokens], x_blocks[:, :, tokens])
-        nc.sync.dma_start(cos_sb[:], cos_pos)
-        nc.sync.dma_start(sin_sb[:], sin_pos)
+            nc.sync.dma_start(cos_sb[:, tokens], cos_pos[:, tokens])
+            nc.sync.dma_start(sin_sb[:, tokens], sin_pos[:, tokens])
         window_of = {0: load_window(nc, windows, base, 0)}
         nc.sync.dma_start(wk_sb[:], wk.rearrange("(k p) c -> p k c", p=P))
         for block in range(1, AHEAD):
             window_of[block] = load_window(nc, windows, base, block)
 
-        for plain, turned in ((wq_sb, wq_turned), (wk_sb, wk_turned)):
+        for projection, (plain, turned) in enumerate(((wq_sb, wq_turned), (wk_sb, wk_turned))):
             source = plain[:].rearrange("p k (h t e) -> p (k h) t e", t=2, e=HALF)
             landing = turned[:].rearrange("p k (h t e) -> p (k h) t e", t=2, e=HALF)
-            nc.vector.tensor_scalar_mul(landing[:, :, 0, :], source[:, :, 1, :], -1.0)
-            nc.vector.tensor_copy(landing[:, :, 1, :], source[:, :, 0, :])
+            nc.scalar.activation(landing[:, :, 0, :], source[:, :, 1, :], COPY, scale=-1.0)
+            nc.scalar.activation(landing[:, :, 1, :], source[:, :, 0, :], COPY)
 
-        for block in range(BLOCKS):
-            plain, turned = ((wq_sb, wq_turned), (wk_sb, wk_turned))[block // HEADS]
-            head = block % HEADS
-            channels = slice(head * P, (head + 1) * P)
-            if block + AHEAD < BLOCKS:
-                window_of[block + AHEAD] = load_window(nc, windows, base, block + AHEAD)
+            for head in range(HEADS):
+                block = projection * HEADS + head
+                channels = slice(head * P, (head + 1) * P)
+                if block + AHEAD < BLOCKS:
+                    window_of[block + AHEAD] = load_window(nc, windows, base, block + AHEAD)
 
-            pair = []
-            for weights, table in ((plain, cos_sb), (turned, sin_sb)):
-                projected = staged.tile([P, N], F32, name="projected")
+                with_cos = products.tile([P, N], F32, name="with_cos")
+                with_sin = products.tile([P, N], F32, name="with_sin")
                 for chunk in range(CHUNKS):
                     tokens = slice(chunk * CHUNK, (chunk + 1) * CHUNK)
-                    bank = banks.tile([P, CHUNK], F32, name="bank")
-                    for k in range(K_BLOCKS):
-                        nc.tensor.matmul(
-                            bank[:],
-                            weights[:, k, channels],
-                            x_sb[:, k, tokens],
-                            start=(k == 0),
-                            stop=(k == K_BLOCKS - 1),
-                        )
-                    nc.scalar.activation(projected[:, tokens], bank[:], COPY)
-                product = staged.tile([P, N], F32, name="product")
-                nc.gpsimd.tensor_tensor(product[:], projected[:], table[:], MULT)
-                pair.append(product)
+                    for weights, table, product in ((plain, cos_sb, with_cos), (turned, sin_sb, with_sin)):
+                        bank = banks.tile([P, CHUNK], F32, name="bank")
+                        for k in range(K_BLOCKS):
+                            nc.tensor.matmul(
+                                bank[:],
+                                weights[:, k, channels],
+                                x_sb[:, k, tokens],
+                                start=(k == 0),
+                                stop=(k == K_BLOCKS - 1),
+                            )
+                        nc.vector.tensor_tensor(product[:, tokens], bank[:], table[:, tokens], MULT)
 
-            window = window_of[block]
-            nc.vector.tensor_tensor(window[:].indirect(offsets[:]), pair[0][:], pair[1][:], ADD)
-            nc.sync.dma_start(out[block * P : (block + 1) * P, :], window[:])
+                window = window_of[block]
+                nc.vector.tensor_tensor(window[:].indirect(offsets[:]), with_cos[:], with_sin[:], ADD)
+                nc.sync.dma_start(out[block * P : (block + 1) * P, :], window[:])

@@ -14,6 +14,7 @@ HEADS = D // P
 BLOCKS = 2 * HEADS
 CHUNK = 512
 CHUNKS = N // CHUNK
+GPSIMD_CHUNK = 0
 AHEAD = 3
 
 FLOPS = 2 * D * (2 * D) * N + 3 * (2 * D) * N
@@ -31,6 +32,7 @@ def tile_flaxllamaattention_b_kernel(tc, x, wq, wk, cos_pos, sin_pos, base, offs
         tc.tile_pool(name="held", bufs=1) as held,
         tc.tile_pool(name="windows", bufs=AHEAD + 1) as windows,
         tc.tile_pool(name="products", bufs=2) as products,
+        tc.tile_pool(name="copies", bufs=4) as copies,
         tc.psum_pool(name="banks", bufs=8) as banks,
     ):
         offsets = held.tile([P, N // 16], U16, name="offsets")
@@ -82,7 +84,12 @@ def tile_flaxllamaattention_b_kernel(tc, x, wq, wk, cos_pos, sin_pos, base, offs
                                 start=(k == 0),
                                 stop=(k == K_BLOCKS - 1),
                             )
-                        nc.vector.tensor_tensor(product[:, tokens], bank[:], table[:, tokens], MULT)
+                        if chunk == GPSIMD_CHUNK:
+                            copied = copies.tile([P, CHUNK], F32, name="copied")
+                            nc.scalar.activation(copied[:], bank[:], COPY)
+                            nc.gpsimd.tensor_tensor(product[:, tokens], copied[:], table[:, tokens], MULT)
+                        else:
+                            nc.vector.tensor_tensor(product[:, tokens], bank[:], table[:, tokens], MULT)
 
                 window = window_of[block]
                 nc.vector.tensor_tensor(window[:].indirect(offsets[:]), with_cos[:], with_sin[:], ADD)

@@ -10,19 +10,26 @@ HALF = 64
 N = 2048
 S = 4096
 K_BLOCKS = D // P
-HEADS = D // P
-BLOCKS = 2 * HEADS
+PAIRS_EACH = D // (2 * P)
+PAIRS = 2 * PAIRS_EACH
+LOW, HIGH = 0, 1
 CHUNK = 512
 CHUNKS = N // CHUNK
 GPSIMD_CHUNK = 0
-AHEAD = 3
+MINUS_SIN, COS, SIN = 0, 1, 2
 
 FLOPS = 2 * D * (2 * D) * N + 3 * (2 * D) * N
 
 
-def load_window(nc, windows, base, block):
+def half_rows(dram, pair, half, head):
+    first = (2 * pair + head) * P + half * HALF
+    return dram[first : first + HALF, :]
+
+
+def load_window(nc, windows, base, pair, half):
     window = windows.tile([P, S], F32, name="window")
-    nc.sync.dma_start(window[:], base[block * P : (block + 1) * P, :])
+    for head in range(2):
+        nc.sync.dma_start(window[head::2, :], half_rows(base, pair, half, head))
     return window
 
 
@@ -30,8 +37,8 @@ def tile_flaxllamaattention_b_kernel(tc, x, wq, wk, cos_pos, sin_pos, base, offs
     nc = tc.nc
     with (
         tc.tile_pool(name="held", bufs=1) as held,
-        tc.tile_pool(name="windows", bufs=AHEAD + 1) as windows,
-        tc.tile_pool(name="products", bufs=2) as products,
+        tc.tile_pool(name="windows", bufs=4) as windows,
+        tc.tile_pool(name="products", bufs=1) as products,
         tc.tile_pool(name="copies", bufs=4) as copies,
         tc.psum_pool(name="banks", bufs=8) as banks,
     ):
@@ -39,58 +46,72 @@ def tile_flaxllamaattention_b_kernel(tc, x, wq, wk, cos_pos, sin_pos, base, offs
         nc.sync.dma_start(offsets[:], offs)
 
         x_sb = held.tile([P, K_BLOCKS, N], BF16, name="x_sb")
-        cos_sb = held.tile([P, N], F32, name="cos_sb")
-        sin_sb = held.tile([P, N], F32, name="sin_sb")
+        tables = held.tile([P, CHUNKS, 3, CHUNK], F32, name="tables")
         wq_sb = held.tile([P, K_BLOCKS, D], BF16, name="wq_sb")
         wk_sb = held.tile([P, K_BLOCKS, D], BF16, name="wk_sb")
-        wq_turned = held.tile([P, K_BLOCKS, D], BF16, name="wq_turned")
-        wk_turned = held.tile([P, K_BLOCKS, D], BF16, name="wk_turned")
+        wq_halves = held.tile([P, 2, K_BLOCKS, PAIRS_EACH, P], BF16, name="wq_halves")
+        wk_halves = held.tile([P, 2, K_BLOCKS, PAIRS_EACH, P], BF16, name="wk_halves")
 
         x_blocks = x.rearrange("(k p) n -> p k n", p=P)
         nc.sync.dma_start(wq_sb[:], wq.rearrange("(k p) c -> p k c", p=P))
         for chunk in range(CHUNKS):
             tokens = slice(chunk * CHUNK, (chunk + 1) * CHUNK)
             nc.sync.dma_start(x_sb[:, :, tokens], x_blocks[:, :, tokens])
-            nc.sync.dma_start(cos_sb[:, tokens], cos_pos[:, tokens])
-            nc.sync.dma_start(sin_sb[:, tokens], sin_pos[:, tokens])
-        window_of = {0: load_window(nc, windows, base, 0)}
+            for head in range(2):
+                rows = slice(head * HALF, (head + 1) * HALF)
+                nc.sync.dma_start(tables[head::2, chunk, SIN, :], sin_pos[rows, tokens])
+                nc.sync.dma_start(tables[head::2, chunk, COS, :], cos_pos[rows, tokens])
+            nc.scalar.activation(tables[:, chunk, MINUS_SIN, :], tables[:, chunk, SIN, :], COPY, scale=-1.0)
+        window_of = {}
+        for half in (LOW, HIGH):
+            window_of[(0, half)] = load_window(nc, windows, base, 0, half)
         nc.sync.dma_start(wk_sb[:], wk.rearrange("(k p) c -> p k c", p=P))
-        for block in range(1, AHEAD):
-            window_of[block] = load_window(nc, windows, base, block)
+        for half in (LOW, HIGH):
+            window_of[(1, half)] = load_window(nc, windows, base, 1, half)
 
-        for projection, (plain, turned) in enumerate(((wq_sb, wq_turned), (wk_sb, wk_turned))):
-            source = plain[:].rearrange("p k (h t e) -> p (k h) t e", t=2, e=HALF)
-            landing = turned[:].rearrange("p k (h t e) -> p (k h) t e", t=2, e=HALF)
-            nc.scalar.activation(landing[:, :, 0, :], source[:, :, 1, :], COPY, scale=-1.0)
-            nc.scalar.activation(landing[:, :, 1, :], source[:, :, 0, :], COPY)
+        for plain, halves, copy_engine in ((wq_sb, wq_halves, nc.vector), (wk_sb, wk_halves, nc.scalar)):
+            source = plain[:].rearrange("p k (r h t e) -> p t (k r) e h", r=PAIRS_EACH, h=2, t=2)
+            for half in (LOW, HIGH):
+                landing = halves[:, half].rearrange("p k r (e h) -> p (k r) e h", h=2)
+                if copy_engine is nc.vector:
+                    nc.vector.tensor_copy(landing, source[:, half])
+                else:
+                    nc.scalar.activation(landing, source[:, half], COPY)
 
-            for head in range(HEADS):
-                block = projection * HEADS + head
-                channels = slice(head * P, (head + 1) * P)
-                if block + AHEAD < BLOCKS:
-                    window_of[block + AHEAD] = load_window(nc, windows, base, block + AHEAD)
+        for pair in range(PAIRS):
+            halves = (wq_halves, wk_halves)[pair // PAIRS_EACH]
+            pair_here = pair % PAIRS_EACH
 
-                with_cos = products.tile([P, N], F32, name="with_cos")
-                with_sin = products.tile([P, N], F32, name="with_sin")
-                for chunk in range(CHUNKS):
-                    tokens = slice(chunk * CHUNK, (chunk + 1) * CHUNK)
-                    for weights, table, product in ((plain, cos_sb, with_cos), (turned, sin_sb, with_sin)):
-                        bank = banks.tile([P, CHUNK], F32, name="bank")
-                        for k in range(K_BLOCKS):
-                            nc.tensor.matmul(
-                                bank[:],
-                                weights[:, k, channels],
-                                x_sb[:, k, tokens],
-                                start=(k == 0),
-                                stop=(k == K_BLOCKS - 1),
-                            )
-                        if chunk == GPSIMD_CHUNK:
-                            copied = copies.tile([P, CHUNK], F32, name="copied")
-                            nc.scalar.activation(copied[:], bank[:], COPY)
-                            nc.gpsimd.tensor_tensor(product[:, tokens], copied[:], table[:, tokens], MULT)
-                        else:
-                            nc.vector.tensor_tensor(product[:, tokens], bank[:], table[:, tokens], MULT)
+            product = products.tile([P, 4, N], F32, name="product")
+            for chunk in range(CHUNKS):
+                tokens = slice(chunk * CHUNK, (chunk + 1) * CHUNK)
+                for half, first_table in ((LOW, COS), (HIGH, MINUS_SIN)):
+                    bank = banks.tile([P, CHUNK], F32, name="bank")
+                    for k in range(K_BLOCKS):
+                        nc.tensor.matmul(
+                            bank[:],
+                            halves[:, half, k, pair_here, :],
+                            x_sb[:, k, tokens],
+                            start=(k == 0),
+                            stop=(k == K_BLOCKS - 1),
+                        )
+                    two_tables = tables[:, chunk, first_table : first_table + 2, :]
+                    two_products = product[:, 2 * half : 2 * half + 2, tokens]
+                    if chunk == GPSIMD_CHUNK:
+                        copied = copies.tile([P, CHUNK], F32, name="copied")
+                        nc.scalar.activation(copied[:], bank[:], COPY)
+                        twice = copied[:].unsqueeze(1).to_broadcast([P, 2, CHUNK])
+                        nc.gpsimd.tensor_tensor(two_products, twice, two_tables, MULT)
+                    else:
+                        twice = bank[:].unsqueeze(1).to_broadcast([P, 2, CHUNK])
+                        nc.vector.tensor_tensor(two_products, twice, two_tables, MULT)
 
-                window = window_of[block]
-                nc.vector.tensor_tensor(window[:].indirect(offsets[:]), with_cos[:], with_sin[:], ADD)
-                nc.sync.dma_start(out[block * P : (block + 1) * P, :], window[:])
+            for half, (plane0, plane1) in ((LOW, (0, 2)), (HIGH, (3, 1))):
+                window = window_of[(pair, half)]
+                nc.vector.tensor_tensor(
+                    window[:].indirect(offsets[:]), product[:, plane0, :], product[:, plane1, :], ADD
+                )
+                for head in range(2):
+                    nc.sync.dma_start(half_rows(out, pair, half, head), window[head::2, :])
+                if pair + 2 < PAIRS:
+                    window_of[(pair + 2, half)] = load_window(nc, windows, base, pair + 2, half)

@@ -15,7 +15,7 @@ PAIRS = 2 * PAIRS_EACH
 LOW, HIGH = 0, 1
 CHUNK = 512
 CHUNKS = N // CHUNK
-GPSIMD_CHUNK = 0
+GPSIMD_TOKENS = N // 3 // 32 * 32
 MINUS_SIN, COS, SIN = 0, 1, 2
 
 FLOPS = 2 * D * (2 * D) * N + 3 * (2 * D) * N
@@ -46,7 +46,7 @@ def tile_flaxllamaattention_b_kernel(tc, x, wq, wk, cos_pos, sin_pos, base, offs
         nc.sync.dma_start(offsets[:], offs)
 
         x_sb = held.tile([P, K_BLOCKS, N], BF16, name="x_sb")
-        tables = held.tile([P, CHUNKS, 3, CHUNK], F32, name="tables")
+        tables = held.tile([P, 3, N], F32, name="tables")
         wq_sb = held.tile([P, K_BLOCKS, D], BF16, name="wq_sb")
         wk_sb = held.tile([P, K_BLOCKS, D], BF16, name="wk_sb")
         wq_halves = held.tile([P, 2, K_BLOCKS, PAIRS_EACH, P], BF16, name="wq_halves")
@@ -59,9 +59,9 @@ def tile_flaxllamaattention_b_kernel(tc, x, wq, wk, cos_pos, sin_pos, base, offs
             nc.sync.dma_start(x_sb[:, :, tokens], x_blocks[:, :, tokens])
             for head in range(2):
                 rows = slice(head * HALF, (head + 1) * HALF)
-                nc.sync.dma_start(tables[head::2, chunk, SIN, :], sin_pos[rows, tokens])
-                nc.sync.dma_start(tables[head::2, chunk, COS, :], cos_pos[rows, tokens])
-            nc.scalar.activation(tables[:, chunk, MINUS_SIN, :], tables[:, chunk, SIN, :], COPY, scale=-1.0)
+                nc.sync.dma_start(tables[head::2, SIN, tokens], sin_pos[rows, tokens])
+                nc.sync.dma_start(tables[head::2, COS, tokens], cos_pos[rows, tokens])
+            nc.scalar.activation(tables[:, MINUS_SIN, tokens], tables[:, SIN, tokens], COPY, scale=-1.0)
         window_of = {}
         for half in (LOW, HIGH):
             window_of[(0, half)] = load_window(nc, windows, base, 0, half)
@@ -83,28 +83,37 @@ def tile_flaxllamaattention_b_kernel(tc, x, wq, wk, cos_pos, sin_pos, base, offs
             pair_here = pair % PAIRS_EACH
 
             product = products.tile([P, 4, N], F32, name="product")
+            copied = {half: copies.tile([P, GPSIMD_TOKENS], F32, name="copied") for half in (LOW, HIGH)}
             for chunk in range(CHUNKS):
-                tokens = slice(chunk * CHUNK, (chunk + 1) * CHUNK)
+                first = chunk * CHUNK
+                for_gpsimd = min(max(GPSIMD_TOKENS - first, 0), CHUNK)
                 for half, first_table in ((LOW, COS), (HIGH, MINUS_SIN)):
                     bank = banks.tile([P, CHUNK], F32, name="bank")
                     for k in range(K_BLOCKS):
                         nc.tensor.matmul(
                             bank[:],
                             halves[:, half, k, pair_here, :],
-                            x_sb[:, k, tokens],
+                            x_sb[:, k, first : first + CHUNK],
                             start=(k == 0),
                             stop=(k == K_BLOCKS - 1),
                         )
-                    two_tables = tables[:, chunk, first_table : first_table + 2, :]
-                    two_products = product[:, 2 * half : 2 * half + 2, tokens]
-                    if chunk == GPSIMD_CHUNK:
-                        copied = copies.tile([P, CHUNK], F32, name="copied")
-                        nc.scalar.activation(copied[:], bank[:], COPY)
-                        twice = copied[:].unsqueeze(1).to_broadcast([P, 2, CHUNK])
-                        nc.gpsimd.tensor_tensor(two_products, twice, two_tables, MULT)
-                    else:
-                        twice = bank[:].unsqueeze(1).to_broadcast([P, 2, CHUNK])
-                        nc.vector.tensor_tensor(two_products, twice, two_tables, MULT)
+                    two_tables = tables[:, first_table : first_table + 2, :]
+                    two_products = product[:, 2 * half : 2 * half + 2, :]
+                    if for_gpsimd > 0:
+                        nc.scalar.activation(
+                            copied[half][:, first : first + for_gpsimd], bank[:, 0:for_gpsimd], COPY
+                        )
+                    if first < GPSIMD_TOKENS <= first + CHUNK:
+                        twice = copied[half][:].unsqueeze(1).to_broadcast([P, 2, GPSIMD_TOKENS])
+                        nc.gpsimd.tensor_tensor(
+                            two_products[:, :, 0:GPSIMD_TOKENS], twice, two_tables[:, :, 0:GPSIMD_TOKENS], MULT
+                        )
+                    if for_gpsimd < CHUNK:
+                        for_vector = slice(first + for_gpsimd, first + CHUNK)
+                        twice = bank[:, for_gpsimd:CHUNK].unsqueeze(1).to_broadcast([P, 2, CHUNK - for_gpsimd])
+                        nc.vector.tensor_tensor(
+                            two_products[:, :, for_vector], twice, two_tables[:, :, for_vector], MULT
+                        )
 
             for half, (plane0, plane1) in ((LOW, (0, 2)), (HIGH, (3, 1))):
                 window = window_of[(pair, half)]

@@ -47,13 +47,23 @@ def tile_flaxllamaattention_b_kernel(tc, x, wq, wk, cos_pos, sin_pos, base, offs
 
         x_sb = held.tile([P, K_BLOCKS, N], BF16, name="x_sb")
         tables = held.tile([P, 3, N], F32, name="tables")
-        wq_sb = held.tile([P, K_BLOCKS, D], BF16, name="wq_sb")
-        wk_sb = held.tile([P, K_BLOCKS, D], BF16, name="wk_sb")
-        wq_halves = held.tile([P, 2, K_BLOCKS, PAIRS_EACH, P], BF16, name="wq_halves")
-        wk_halves = held.tile([P, 2, K_BLOCKS, PAIRS_EACH, P], BF16, name="wk_halves")
+        w_sb = held.tile([P, PAIRS, K_BLOCKS, 2 * P], BF16, name="w_sb")
+        w_halves = held.tile([P, PAIRS, 2, K_BLOCKS, P], BF16, name="w_halves")
+
+        def load_weights(pair):
+            w_blocks = (wq, wk)[pair // PAIRS_EACH].rearrange("(k p) c -> p k c", p=P)
+            first = (pair % PAIRS_EACH) * 2 * P
+            nc.sync.dma_start(w_sb[:, pair], w_blocks[:, :, first : first + 2 * P])
+            source = w_sb[:, pair].rearrange("p k (h t e) -> p t k e h", h=2, t=2)
+            for half in (LOW, HIGH):
+                landing = w_halves[:, pair, half].rearrange("p k (e h) -> p k e h", h=2)
+                if pair == 0 and half == LOW:
+                    nc.vector.tensor_copy(landing, source[:, half])
+                else:
+                    nc.scalar.activation(landing, source[:, half], COPY)
 
         x_blocks = x.rearrange("(k p) n -> p k n", p=P)
-        nc.sync.dma_start(wq_sb[:], wq.rearrange("(k p) c -> p k c", p=P))
+        load_weights(0)
         for chunk in range(CHUNKS):
             tokens = slice(chunk * CHUNK, (chunk + 1) * CHUNK)
             nc.sync.dma_start(x_sb[:, :, tokens], x_blocks[:, :, tokens])
@@ -63,36 +73,26 @@ def tile_flaxllamaattention_b_kernel(tc, x, wq, wk, cos_pos, sin_pos, base, offs
                 nc.sync.dma_start(tables[head::2, COS, tokens], cos_pos[rows, tokens])
             nc.scalar.activation(tables[:, MINUS_SIN, tokens], tables[:, SIN, tokens], COPY, scale=-1.0)
         window_of = {}
-        for half in (LOW, HIGH):
-            window_of[(0, half)] = load_window(nc, windows, base, 0, half)
-        nc.sync.dma_start(wk_sb[:], wk.rearrange("(k p) c -> p k c", p=P))
-        for half in (LOW, HIGH):
-            window_of[(1, half)] = load_window(nc, windows, base, 1, half)
-
-        for plain, halves, copy_engine in ((wq_sb, wq_halves, nc.vector), (wk_sb, wk_halves, nc.scalar)):
-            source = plain[:].rearrange("p k (r h t e) -> p t (k r) e h", r=PAIRS_EACH, h=2, t=2)
+        for pair in range(2):
             for half in (LOW, HIGH):
-                landing = halves[:, half].rearrange("p k r (e h) -> p (k r) e h", h=2)
-                if copy_engine is nc.vector:
-                    nc.vector.tensor_copy(landing, source[:, half])
-                else:
-                    nc.scalar.activation(landing, source[:, half], COPY)
+                window_of[(pair, half)] = load_window(nc, windows, base, pair, half)
+            load_weights(pair + 1)
+        load_weights(3)
 
         for pair in range(PAIRS):
-            halves = (wq_halves, wk_halves)[pair // PAIRS_EACH]
-            pair_here = pair % PAIRS_EACH
+            gpsimd_tokens = CHUNK if pair == 0 else GPSIMD_TOKENS
 
             product = products.tile([P, 4, N], F32, name="product")
             copied = {half: copies.tile([P, GPSIMD_TOKENS], F32, name="copied") for half in (LOW, HIGH)}
             for chunk in range(CHUNKS):
                 first = chunk * CHUNK
-                for_gpsimd = min(max(GPSIMD_TOKENS - first, 0), CHUNK)
+                for_gpsimd = min(max(gpsimd_tokens - first, 0), CHUNK)
                 for half, first_table in ((LOW, COS), (HIGH, MINUS_SIN)):
                     bank = banks.tile([P, CHUNK], F32, name="bank")
                     for k in range(K_BLOCKS):
                         nc.tensor.matmul(
                             bank[:],
-                            halves[:, half, k, pair_here, :],
+                            w_halves[:, pair, half, k, :],
                             x_sb[:, k, first : first + CHUNK],
                             start=(k == 0),
                             stop=(k == K_BLOCKS - 1),
@@ -103,10 +103,10 @@ def tile_flaxllamaattention_b_kernel(tc, x, wq, wk, cos_pos, sin_pos, base, offs
                         nc.scalar.activation(
                             copied[half][:, first : first + for_gpsimd], bank[:, 0:for_gpsimd], COPY
                         )
-                    if first < GPSIMD_TOKENS <= first + CHUNK:
-                        twice = copied[half][:].unsqueeze(1).to_broadcast([P, 2, GPSIMD_TOKENS])
+                    if first < gpsimd_tokens <= first + CHUNK:
+                        twice = copied[half][:, 0:gpsimd_tokens].unsqueeze(1).to_broadcast([P, 2, gpsimd_tokens])
                         nc.gpsimd.tensor_tensor(
-                            two_products[:, :, 0:GPSIMD_TOKENS], twice, two_tables[:, :, 0:GPSIMD_TOKENS], MULT
+                            two_products[:, :, 0:gpsimd_tokens], twice, two_tables[:, :, 0:gpsimd_tokens], MULT
                         )
                     if for_gpsimd < CHUNK:
                         for_vector = slice(first + for_gpsimd, first + CHUNK)

@@ -67,11 +67,13 @@ def tile_flaxllamaattention_b_kernel(tc, x, wq, wk, cos_pos, sin_pos, base, offs
         for chunk in range(CHUNKS):
             tokens = slice(chunk * CHUNK, (chunk + 1) * CHUNK)
             nc.sync.dma_start(x_sb[:, :, tokens], x_blocks[:, :, tokens])
-            for head in range(2):
-                rows = slice(head * HALF, (head + 1) * HALF)
-                nc.sync.dma_start(tables[head::2, SIN, tokens], sin_pos[rows, tokens])
-                nc.sync.dma_start(tables[head::2, COS, tokens], cos_pos[rows, tokens])
-            nc.scalar.activation(tables[:, MINUS_SIN, tokens], tables[:, SIN, tokens], COPY, scale=-1.0)
+            if chunk % 2 == 0:
+                tokens = slice(chunk * CHUNK, (chunk + 2) * CHUNK)
+                for head in range(2):
+                    rows = slice(head * HALF, (head + 1) * HALF)
+                    nc.sync.dma_start(tables[head::2, SIN, tokens], sin_pos[rows, tokens])
+                    nc.sync.dma_start(tables[head::2, COS, tokens], cos_pos[rows, tokens])
+                nc.scalar.activation(tables[:, MINUS_SIN, tokens], tables[:, SIN, tokens], COPY, scale=-1.0)
         window_of = {}
         for pair in range(2):
             for half in (LOW, HIGH):

@@ -57,10 +57,7 @@ def tile_flaxllamaattention_b_kernel(tc, x, wq, wk, cos_pos, sin_pos, base, offs
             source = w_sb[:, pair].rearrange("p k (h t e) -> p t k e h", h=2, t=2)
             for half in (LOW, HIGH):
                 landing = w_halves[:, pair, half].rearrange("p k (e h) -> p k e h", h=2)
-                if pair == 0 and half == LOW:
-                    nc.vector.tensor_copy(landing, source[:, half])
-                else:
-                    nc.scalar.activation(landing, source[:, half], COPY)
+                nc.scalar.activation(landing, source[:, half], COPY)
 
         x_blocks = x.rearrange("(k p) n -> p k n", p=P)
         load_weights(0)
@@ -82,13 +79,11 @@ def tile_flaxllamaattention_b_kernel(tc, x, wq, wk, cos_pos, sin_pos, base, offs
         load_weights(3)
 
         for pair in range(PAIRS):
-            gpsimd_tokens = CHUNK if pair == 0 else GPSIMD_TOKENS
-
             product = products.tile([P, 4, N], F32, name="product")
             copied = {half: copies.tile([P, GPSIMD_TOKENS], F32, name="copied") for half in (LOW, HIGH)}
             for chunk in range(CHUNKS):
                 first = chunk * CHUNK
-                for_gpsimd = min(max(gpsimd_tokens - first, 0), CHUNK)
+                for_gpsimd = min(max(GPSIMD_TOKENS - first, 0), CHUNK)
                 for half, first_table in ((LOW, COS), (HIGH, MINUS_SIN)):
                     bank = banks.tile([P, CHUNK], F32, name="bank")
                     for k in range(K_BLOCKS):
@@ -105,10 +100,10 @@ def tile_flaxllamaattention_b_kernel(tc, x, wq, wk, cos_pos, sin_pos, base, offs
                         nc.scalar.activation(
                             copied[half][:, first : first + for_gpsimd], bank[:, 0:for_gpsimd], COPY
                         )
-                    if first < gpsimd_tokens <= first + CHUNK:
-                        twice = copied[half][:, 0:gpsimd_tokens].unsqueeze(1).to_broadcast([P, 2, gpsimd_tokens])
+                    if first < GPSIMD_TOKENS <= first + CHUNK:
+                        twice = copied[half][:].unsqueeze(1).to_broadcast([P, 2, GPSIMD_TOKENS])
                         nc.gpsimd.tensor_tensor(
-                            two_products[:, :, 0:gpsimd_tokens], twice, two_tables[:, :, 0:gpsimd_tokens], MULT
+                            two_products[:, :, 0:GPSIMD_TOKENS], twice, two_tables[:, :, 0:GPSIMD_TOKENS], MULT
                         )
                     if for_gpsimd < CHUNK:
                         for_vector = slice(first + for_gpsimd, first + CHUNK)

@@ -38,7 +38,7 @@ def tile_flaxllamaattention_b_kernel(tc, x, wq, wk, cos_pos, sin_pos, base, offs
     with (
         tc.tile_pool(name="held", bufs=1) as held,
         tc.tile_pool(name="windows", bufs=4) as windows,
-        tc.tile_pool(name="products", bufs=1) as products,
+        tc.tile_pool(name="products", bufs=2) as products,
         tc.tile_pool(name="copies", bufs=4) as copies,
         tc.psum_pool(name="banks", bufs=8) as banks,
     ):

@@ -15,7 +15,7 @@ PAIRS = 2 * PAIRS_EACH
 LOW, HIGH = 0, 1
 CHUNK = 512
 CHUNKS = N // CHUNK
-GPSIMD_TOKENS = N // 3 // 32 * 32
+GPSIMD_TOKENS = N // 3 // 128 * 128
 MINUS_SIN, COS, SIN = 0, 1, 2
 
 FLOPS = 2 * D * (2 * D) * N + 3 * (2 * D) * N

@@ -15,7 +15,9 @@ PAIRS = 2 * PAIRS_EACH
 LOW, HIGH = 0, 1
 CHUNK = 512
 CHUNKS = N // CHUNK
-GPSIMD_TOKENS = N // 3 // 128 * 128
+SPAN = 2 * CHUNK
+SPANS = N // SPAN
+GPSIMD_TOKENS = SPAN // 3 // 64 * 64
 MINUS_SIN, COS, SIN = 0, 1, 2
 
 FLOPS = 2 * D * (2 * D) * N + 3 * (2 * D) * N
@@ -39,7 +41,7 @@ def tile_flaxllamaattention_b_kernel(tc, x, wq, wk, cos_pos, sin_pos, base, offs
         tc.tile_pool(name="held", bufs=1) as held,
         tc.tile_pool(name="windows", bufs=4) as windows,
         tc.tile_pool(name="products", bufs=2) as products,
-        tc.tile_pool(name="copies", bufs=4) as copies,
+        tc.tile_pool(name="copies", bufs=8) as copies,
         tc.psum_pool(name="banks", bufs=8) as banks,
     ):
         offsets = held.tile([P, N // 16], U16, name="offsets")
@@ -65,7 +67,7 @@ def tile_flaxllamaattention_b_kernel(tc, x, wq, wk, cos_pos, sin_pos, base, offs
             tokens = slice(chunk * CHUNK, (chunk + 1) * CHUNK)
             nc.sync.dma_start(x_sb[:, :, tokens], x_blocks[:, :, tokens])
             if chunk % 2 == 0:
-                tokens = slice(chunk * CHUNK, (chunk + 2) * CHUNK)
+                tokens = slice(chunk * CHUNK, chunk * CHUNK + SPAN)
                 for head in range(2):
                     rows = slice(head * HALF, (head + 1) * HALF)
                     nc.sync.dma_start(tables[head::2, SIN, tokens], sin_pos[rows, tokens])
@@ -80,10 +82,9 @@ def tile_flaxllamaattention_b_kernel(tc, x, wq, wk, cos_pos, sin_pos, base, offs
 
         for pair in range(PAIRS):
             product = products.tile([P, 4, N], F32, name="product")
-            copied = {half: copies.tile([P, GPSIMD_TOKENS], F32, name="copied") for half in (LOW, HIGH)}
             for chunk in range(CHUNKS):
                 first = chunk * CHUNK
-                for_gpsimd = min(max(GPSIMD_TOKENS - first, 0), CHUNK)
+                for_gpsimd = GPSIMD_TOKENS if first % SPAN == 0 else 0
                 for half, first_table in ((LOW, COS), (HIGH, MINUS_SIN)):
                     bank = banks.tile([P, CHUNK], F32, name="bank")
                     for k in range(K_BLOCKS):
@@ -97,20 +98,14 @@ def tile_flaxllamaattention_b_kernel(tc, x, wq, wk, cos_pos, sin_pos, base, offs
                     two_tables = tables[:, first_table : first_table + 2, :]
                     two_products = product[:, 2 * half : 2 * half + 2, :]
                     if for_gpsimd > 0:
-                        nc.scalar.activation(
-                            copied[half][:, first : first + for_gpsimd], bank[:, 0:for_gpsimd], COPY
-                        )
-                    if first < GPSIMD_TOKENS <= first + CHUNK:
-                        twice = copied[half][:].unsqueeze(1).to_broadcast([P, 2, GPSIMD_TOKENS])
-                        nc.gpsimd.tensor_tensor(
-                            two_products[:, :, 0:GPSIMD_TOKENS], twice, two_tables[:, :, 0:GPSIMD_TOKENS], MULT
-                        )
-                    if for_gpsimd < CHUNK:
-                        for_vector = slice(first + for_gpsimd, first + CHUNK)
-                        twice = bank[:, for_gpsimd:CHUNK].unsqueeze(1).to_broadcast([P, 2, CHUNK - for_gpsimd])
-                        nc.vector.tensor_tensor(
-                            two_products[:, :, for_vector], twice, two_tables[:, :, for_vector], MULT
-                        )
+                        copied = copies.tile([P, GPSIMD_TOKENS], F32, name="copied")
+                        nc.scalar.activation(copied[:], bank[:, 0:for_gpsimd], COPY)
+                        tokens = slice(first, first + for_gpsimd)
+                        twice = copied[:].unsqueeze(1).to_broadcast([P, 2, for_gpsimd])
+                        nc.gpsimd.tensor_tensor(two_products[:, :, tokens], twice, two_tables[:, :, tokens], MULT)
+                    tokens = slice(first + for_gpsimd, first + CHUNK)
+                    twice = bank[:, for_gpsimd:CHUNK].unsqueeze(1).to_broadcast([P, 2, CHUNK - for_gpsimd])
+                    nc.vector.tensor_tensor(two_products[:, :, tokens], twice, two_tables[:, :, tokens], MULT)
 
             for half, (plane0, plane1) in ((LOW, (0, 2)), (HIGH, (3, 1))):
                 window = window_of[(pair, half)]

@@ -16,7 +16,6 @@ LOW, HIGH = 0, 1
 CHUNK = 512
 CHUNKS = N // CHUNK
 SPAN = 2 * CHUNK
-SPANS = N // SPAN
 GPSIMD_TOKENS = SPAN // 3 // 64 * 64
 MINUS_SIN, COS, SIN = 0, 1, 2
 
@@ -63,16 +62,22 @@ def tile_flaxllamaattention_b_kernel(tc, x, wq, wk, cos_pos, sin_pos, base, offs
 
         x_blocks = x.rearrange("(k p) n -> p k n", p=P)
         load_weights(0)
-        for chunk in range(CHUNKS):
-            tokens = slice(chunk * CHUNK, (chunk + 1) * CHUNK)
-            nc.sync.dma_start(x_sb[:, :, tokens], x_blocks[:, :, tokens])
-            if chunk % 2 == 0:
-                tokens = slice(chunk * CHUNK, chunk * CHUNK + SPAN)
-                for head in range(2):
-                    rows = slice(head * HALF, (head + 1) * HALF)
-                    nc.sync.dma_start(tables[head::2, SIN, tokens], sin_pos[rows, tokens])
-                    nc.sync.dma_start(tables[head::2, COS, tokens], cos_pos[rows, tokens])
-                nc.scalar.activation(tables[:, MINUS_SIN, tokens], tables[:, SIN, tokens], COPY, scale=-1.0)
+        def load_x(first, last):
+            nc.sync.dma_start(x_sb[:, :, first:last], x_blocks[:, :, first:last])
+
+        def load_tables(span):
+            tokens = slice(span * SPAN, (span + 1) * SPAN)
+            for head in range(2):
+                rows = slice(head * HALF, (head + 1) * HALF)
+                nc.sync.dma_start(tables[head::2, SIN, tokens], sin_pos[rows, tokens])
+                nc.sync.dma_start(tables[head::2, COS, tokens], cos_pos[rows, tokens])
+            nc.scalar.activation(tables[:, MINUS_SIN, tokens], tables[:, SIN, tokens], COPY, scale=-1.0)
+
+        load_x(0, CHUNK)
+        load_tables(0)
+        load_x(CHUNK, SPAN)
+        load_x(SPAN, N)
+        load_tables(1)
         window_of = {}
         for pair in range(2):
             for half in (LOW, HIGH):

@@ -71,7 +71,7 @@ def tile_flaxllamaattention_b_kernel(tc, x, wq, wk, cos_pos, sin_pos, base, offs
                 rows = slice(head * HALF, (head + 1) * HALF)
                 nc.sync.dma_start(tables[head::2, SIN, tokens], sin_pos[rows, tokens])
                 nc.sync.dma_start(tables[head::2, COS, tokens], cos_pos[rows, tokens])
-            nc.scalar.activation(tables[:, MINUS_SIN, tokens], tables[:, SIN, tokens], COPY, scale=-1.0)
+            nc.vector.tensor_scalar(tables[:, MINUS_SIN, tokens], tables[:, SIN, tokens], -1.0, None, op0=MULT)
 
         load_x(0, CHUNK)
         load_tables(0)

import concourse.mybir as mybir

BF16, F32, U16 = mybir.dt.bfloat16, mybir.dt.float32, mybir.dt.uint16
MULT, ADD = mybir.AluOpType.mult, mybir.AluOpType.add
COPY = mybir.ActivationFunctionType.Copy

P = 128
D = 512
HALF = 64
N = 2048
S = 4096
K_BLOCKS = D // P
PAIRS_EACH = D // (2 * P)
PAIRS = 2 * PAIRS_EACH
LOW, HIGH = 0, 1
CHUNK = 512
CHUNKS = N // CHUNK
SPAN = 2 * CHUNK
GPSIMD_TOKENS = SPAN // 3 // 64 * 64
MINUS_SIN, COS, SIN = 0, 1, 2

FLOPS = 2 * D * (2 * D) * N + 3 * (2 * D) * N


def half_rows(dram, pair, half, head):
    first = (2 * pair + head) * P + half * HALF
    return dram[first : first + HALF, :]


def load_window(nc, windows, base, pair, half):
    window = windows.tile([P, S], F32, name="window")
    for head in range(2):
        nc.sync.dma_start(window[head::2, :], half_rows(base, pair, half, head))
    return window


def tile_flaxllamaattention_b_kernel(tc, x, wq, wk, cos_pos, sin_pos, base, offs, out):
    nc = tc.nc
    with (
        tc.tile_pool(name="held", bufs=1) as held,
        tc.tile_pool(name="windows", bufs=4) as windows,
        tc.tile_pool(name="products", bufs=2) as products,
        tc.tile_pool(name="copies", bufs=8) as copies,
        tc.psum_pool(name="banks", bufs=8) as banks,
    ):
        offsets = held.tile([P, N // 16], U16, name="offsets")
        nc.sync.dma_start(offsets[:], offs)

        x_sb = held.tile([P, K_BLOCKS, N], BF16, name="x_sb")
        tables = held.tile([P, 3, N], F32, name="tables")
        w_sb = held.tile([P, PAIRS, K_BLOCKS, 2 * P], BF16, name="w_sb")
        w_halves = held.tile([P, PAIRS, 2, K_BLOCKS, P], BF16, name="w_halves")

        def load_weights(pair):
            w_blocks = (wq, wk)[pair // PAIRS_EACH].rearrange("(k p) c -> p k c", p=P)
            first = (pair % PAIRS_EACH) * 2 * P
            nc.sync.dma_start(w_sb[:, pair], w_blocks[:, :, first : first + 2 * P])
            source = w_sb[:, pair].rearrange("p k (h t e) -> p t k e h", h=2, t=2)
            for half in (LOW, HIGH):
                landing = w_halves[:, pair, half].rearrange("p k (e h) -> p k e h", h=2)
                nc.scalar.activation(landing, source[:, half], COPY)

        x_blocks = x.rearrange("(k p) n -> p k n", p=P)
        load_weights(0)
        def load_x(first, last):
            nc.sync.dma_start(x_sb[:, :, first:last], x_blocks[:, :, first:last])

        def load_tables(span):
            tokens = slice(span * SPAN, (span + 1) * SPAN)
            for head in range(2):
                rows = slice(head * HALF, (head + 1) * HALF)
                nc.sync.dma_start(tables[head::2, SIN, tokens], sin_pos[rows, tokens])
                nc.sync.dma_start(tables[head::2, COS, tokens], cos_pos[rows, tokens])
            nc.vector.tensor_scalar(tables[:, MINUS_SIN, tokens], tables[:, SIN, tokens], -1.0, None, op0=MULT)

        load_x(0, CHUNK)
        load_tables(0)
        load_x(CHUNK, SPAN)
        load_x(SPAN, N)
        load_tables(1)
        window_of = {}
        for pair in range(2):
            for half in (LOW, HIGH):
                window_of[(pair, half)] = load_window(nc, windows, base, pair, half)
            load_weights(pair + 1)
        load_weights(3)

        for pair in range(PAIRS):
            product = products.tile([P, 4, N], F32, name="product")
            for chunk in range(CHUNKS):
                first = chunk * CHUNK
                for_gpsimd = GPSIMD_TOKENS if first % SPAN == 0 else 0
                for half, first_table in ((LOW, COS), (HIGH, MINUS_SIN)):
                    bank = banks.tile([P, CHUNK], F32, name="bank")
                    for k in range(K_BLOCKS):
                        nc.tensor.matmul(
                            bank[:],
                            w_halves[:, pair, half, k, :],
                            x_sb[:, k, first : first + CHUNK],
                            start=(k == 0),
                            stop=(k == K_BLOCKS - 1),
                        )
                    two_tables = tables[:, first_table : first_table + 2, :]
                    two_products = product[:, 2 * half : 2 * half + 2, :]
                    if for_gpsimd > 0:
                        copied = copies.tile([P, GPSIMD_TOKENS], F32, name="copied")
                        nc.scalar.activation(copied[:], bank[:, 0:for_gpsimd], COPY)
                        tokens = slice(first, first + for_gpsimd)
                        twice = copied[:].unsqueeze(1).to_broadcast([P, 2, for_gpsimd])
                        nc.gpsimd.tensor_tensor(two_products[:, :, tokens], twice, two_tables[:, :, tokens], MULT)
                    tokens = slice(first + for_gpsimd, first + CHUNK)
                    twice = bank[:, for_gpsimd:CHUNK].unsqueeze(1).to_broadcast([P, 2, CHUNK - for_gpsimd])
                    nc.vector.tensor_tensor(two_products[:, :, tokens], twice, two_tables[:, :, tokens], MULT)

            for half, (plane0, plane1) in ((LOW, (0, 2)), (HIGH, (3, 1))):
                window = window_of[(pair, half)]
                nc.vector.tensor_tensor(
                    window[:].indirect(offsets[:]), product[:, plane0, :], product[:, plane1, :], ADD
                )
                for head in range(2):
                    nc.sync.dma_start(half_rows(out, pair, half, head), window[head::2, :])
                if pair + 2 < PAIRS:
                    window_of[(pair + 2, half)] = load_window(nc, windows, base, pair + 2, half)
